import numpy as np
import ml_dtypes


def mxq(x, axis, fmt="e4m3"):
    dtype, down = {"e4m3": (ml_dtypes.float8_e4m3fn, 7), "e5m2": (ml_dtypes.float8_e5m2, 14)}[fmt]
    v = np.moveaxis(np.asarray(x, np.float32).astype(ml_dtypes.bfloat16).astype(np.float64), axis, -1)
    blocks = v.reshape(v.shape[:-1] + (-1, 32))
    amax = np.abs(blocks).max(-1, keepdims=True)
    byte = np.maximum(np.where(amax > 0, np.frexp(amax)[1] - 1 + 127, 0) - down, 1)
    scale = np.exp2(byte - 127.0)
    codes = (blocks / scale).astype(np.float32).astype(dtype).astype(np.float64)
    return np.moveaxis((codes * scale).reshape(v.shape), -1, axis)


WIDE = False


def mx_kscale(k):
    if not WIDE:
        return np.ones(k)
    levels = np.array([10, -10, 5, -5, 0])
    a = np.random.permutation(np.resize(levels, k // 512 * 4)).reshape(k // 512, 4)
    idx = np.arange(k)
    return np.exp2(a[idx // 512, idx % 128 // 32])


BF16 = ml_dtypes.bfloat16


def bf(x):
    return np.asarray(x, np.float32).astype(BF16)


def f64(x):
    return np.asarray(x).astype(np.float64)


E2M1 = np.array([0.0, 0.5, 1.0, 1.5, 2.0, 3.0, 4.0, 6.0, -0.0, -0.5, -1.0, -1.5, -2.0, -3.0, -4.0, -6.0])


def pack_weight(w, fmt):
    k, n = w.shape
    w = f64(bf(w)).reshape(k // 32, 32, n)
    amax = np.abs(w).max(1)
    if fmt == "e4m3":
        byte = np.frexp(amax)[1] - 1 + 127 - 7
    else:
        mant, ex = np.frexp(amax / 6.0)
        byte = np.where(mant > 0.5, ex, ex - 1) + 127
    byte = np.clip(np.where(amax > 0, byte, 1), 1, 254)
    scaled = (w * np.exp2(127.0 - byte)[:, None, :]).reshape(k, n).astype(np.float32)
    by_word = np.ascontiguousarray(scaled.reshape(k // 512, 128, 4, n).transpose(0, 1, 3, 2))
    if fmt == "e4m3":
        words = by_word.astype(ml_dtypes.float8_e4m3fn).view(np.uint8)
    else:
        c = by_word.astype(ml_dtypes.float4_e2m1fn).view(np.uint8) & 0xF
        words = c[..., 0::2] | (c[..., 1::2] << 4)
    return np.ascontiguousarray(words), np.ascontiguousarray(byte.astype(np.uint8).reshape(k // 512, 16, n))


def unpack_weight(words, scales, fmt):
    g, p, n, _ = words.shape
    if fmt == "e4m3":
        vals = np.ascontiguousarray(words).view(ml_dtypes.float8_e4m3fn).astype(np.float64)
    else:
        nib = np.empty((g, p, n, 4), np.uint8)
        nib[..., 0::2] = words & 0xF
        nib[..., 1::2] = words >> 4
        vals = E2M1[nib]
    vals = vals * np.repeat(np.exp2(scales.astype(np.float64) - 127.0), 8, axis=1)[..., None]
    return vals.transpose(0, 1, 3, 2).reshape(g * 512, n)


B, D, C = 128, 128, 1024
EPS_SQRT = 1e-10
EPS_NORM = 1e-12
FMT = "e4m3"


def setup_inputs():
    s = mx_kscale(D * D)
    a = np.round(np.log2(np.array([s.max(), s.min()])) / 2)
    r = np.repeat(np.exp2(a - a.min()), D // 2)
    g = np.exp2(np.round(np.log2(np.mean(r ** 2))))
    feat = bf(np.random.standard_normal((B, D)) * r ** 2)
    w = np.random.standard_normal((C, D * D)) * g / np.outer(r, r).reshape(-1)
    words, scales = pack_weight(np.ascontiguousarray(w.T), FMT)
    b = bf(np.random.standard_normal(C) * 0.3)
    return {"feat": feat,
            "W_words": words,
            "W_scales": scales,
            "b": b}


def reference(feat, W_words, W_scales, b):
    feat = f64(feat)
    x = (feat[:, :, None] * feat[:, None, :]).reshape(feat.shape[0], -1)
    x = np.sign(x) * np.sqrt(np.abs(x) + EPS_SQRT)
    norm = np.maximum(np.linalg.norm(x, axis=1, keepdims=True), EPS_NORM)
    x = x / norm
    return (mxq(x, 1, "e4m3") @ unpack_weight(W_words, W_scales, FMT)) + f64(b)

@@ -1,0 +1,256 @@
+from contextlib import ExitStack
+
+import concourse.mybir as mybir
+from concourse.masks import make_identity
+
+F32 = mybir.dt.float32
+BF16 = mybir.dt.bfloat16
+I32 = mybir.dt.int32
+U32 = mybir.dt.uint32
+U8 = mybir.dt.uint8
+FP8X4 = mybir.dt.float8_e4m3fn_x4
+ALU = mybir.AluOpType
+ACT = mybir.ActivationFunctionType
+AX = mybir.AxisListType
+
+P = 128
+D = 128
+C = 1024
+EPS_SQRT = 1e-10
+EPS_NORM = 1e-12
+
+K_PASS = 512
+ROWS_PASS = K_PASS // D
+PASSES = D * D // K_PASS
+N_TILE = 512
+HALVES = C // N_TILE
+BATCH = 4
+BATCHES = PASSES // BATCH
+ROWS = BATCH * ROWS_PASS
+HALF_D = D // 2
+
+FLOPS = 2 * P * D * D * C
+
+
+def column_of(i):
+    return ((i // 2) % 2) * HALF_D + (i // 4) * 2 + i % 2
+
+
+def tile_bcnnresnet_k_kernel(tc, feat, W_words, W_scales, b, out):
+    nc = tc.nc
+    with ExitStack() as ctx:
+        const = ctx.enter_context(tc.tile_pool(name="const", bufs=1))
+        w_pool = ctx.enter_context(tc.tile_pool(name="w_pool", bufs=PASSES // 2))
+        plane_pool = ctx.enter_context(tc.tile_pool(name="plane_pool", bufs=BATCHES))
+        x_pool = ctx.enter_context(tc.tile_pool(name="x_pool", bufs=BATCHES))
+        work = ctx.enter_context(tc.tile_pool(name="work", bufs=3))
+        psum_acc = ctx.enter_context(tc.psum_pool(name="psum_acc", bufs=1))
+        psum_bias = ctx.enter_context(tc.psum_pool(name="psum_bias", bufs=HALVES))
+        psum_t = ctx.enter_context(tc.psum_pool(name="psum_t", bufs=4))
+        ctx.enter_context(tc.manual_schedule())
+
+        feat_sb = const.tile([P, D], BF16)
+        nc.sync.dma_start(out=feat_sb[:], in_=feat)
+
+        w_planes = []
+        for batch in range(BATCHES):
+            planes = plane_pool.tile([P, C], U8, name="w_planes%d" % batch, tag="w_planes", align_bytes=64)
+            nc.vector.memset(planes[:].bitcast(I32), 0)
+            w_planes.append(planes)
+        bias_rows = const.tile([P, C], BF16)
+        nc.vector.memset(bias_rows[:], 0.0)
+        ones = const.tile([P, P], BF16)
+        nc.vector.memset(ones[:], 1.0)
+        nc.scalar.dma_start(out=bias_rows[0:1, :], in_=b.rearrange("(o c) -> o c", o=1))
+
+        w_words = []
+        for batch in range(BATCHES):
+            for quad in range(4):
+                nc.sync.dma_start(
+                    out=w_planes[batch][32 * quad : 32 * quad + 16, :].bitcast(I32),
+                    in_=W_scales[BATCH * batch : BATCH * (batch + 1), 4 * quad : 4 * quad + 4, :].bitcast(I32),
+                )
+            for pair in range(BATCH // 2):
+                first = BATCH * batch + 2 * pair
+                words = w_pool.tile([P, 2, C], U32, name="w_words%d" % (first // 2), tag="w_words", align_bytes=64)
+                nc.sync.dma_start(
+                    out=words[:].bitcast(I32),
+                    in_=W_words[first : first + 2].rearrange("g p c t -> p g (c t)").bitcast(I32),
+                )
+                w_words.append(words)
+
+        ident = const.tile([P, P], F32)
+        make_identity(nc, ident[:])
+
+        bias_ps = []
+        for half in range(HALVES):
+            spread = psum_bias.tile([P, N_TILE], F32, name="bias_ps%d" % half, tag="bias_ps")
+            nc.tensor.matmul(
+                out=spread[:], lhsT=ones[:], rhs=bias_rows[:, half * N_TILE : (half + 1) * N_TILE], start=True, stop=True
+            )
+            bias_ps.append(spread)
+
+        f_sorted = const.tile([P, D], F32)
+        nc.vector.tensor_copy(
+            out=f_sorted[:].rearrange("n (u h e) -> n u h e", u=2, e=2),
+            in_=feat_sb[:].rearrange("n (h u e) -> n u h e", u=2, e=2),
+        )
+        abs_f = const.tile([P, D], F32)
+        abs_sum = const.tile([P, 1], F32)
+        nc.vector.scalar_tensor_tensor(
+            out=abs_f[:], in0=f_sorted[:], scalar=-1.0, in1=f_sorted[:], op0=ALU.mult, op1=ALU.max, accum_out=abs_sum[:]
+        )
+        nonzero = const.tile([P, D], F32)
+        count = const.tile([P, 1], F32)
+        nc.vector.tensor_scalar(
+            out=nonzero[:], in0=f_sorted[:], scalar1=0.0, scalar2=None, op0=ALU.not_equal, op1=ALU.add, accum_out=count[:]
+        )
+        sum_sq = const.tile([P, 1], F32)
+        nc.vector.tensor_tensor(out=sum_sq[:], in0=abs_sum[:], in1=abs_sum[:], op=ALU.mult)
+        eps_sum = const.tile([P, 1], F32)
+        nc.vector.scalar_tensor_tensor(
+            out=eps_sum[:], in0=count[:], scalar=EPS_SQRT, in1=count[:], op0=ALU.mult, op1=ALU.mult
+        )
+        norm_sq = const.tile([P, 1], F32)
+        nc.vector.tensor_tensor(out=norm_sq[:], in0=sum_sq[:], in1=eps_sum[:], op=ALU.add)
+        norm_sq_clamped = const.tile([P, 1], F32)
+        nc.vector.tensor_scalar_max(out=norm_sq_clamped[:], in0=norm_sq[:], scalar1=EPS_NORM * EPS_NORM)
+        inv_norm_sq = const.tile([P, 1], F32)
+        nc.vector.reciprocal(out=inv_norm_sq[:], in_=norm_sq_clamped[:])
+        abs_scaled = const.tile([P, D], F32)
+        nc.vector.tensor_scalar_mul(out=abs_scaled[:], in0=abs_f[:], scalar1=inv_norm_sq[:, 0:1])
+        eps_scaled = const.tile([P, 1], F32)
+        nc.vector.tensor_scalar_mul(out=eps_scaled[:], in0=inv_norm_sq[:], scalar1=EPS_SQRT)
+
+        is_neg = const.tile([P, D], F32)
+        nc.vector.tensor_scalar(out=is_neg[:], in0=f_sorted[:], scalar1=0.0, scalar2=None, op0=ALU.is_lt)
+        sign_f = const.tile([P, D], F32)
+        nc.vector.scalar_tensor_tensor(
+            out=sign_f[:], in0=f_sorted[:], scalar=0.0, in1=is_neg[:], op0=ALU.is_gt, op1=ALU.subtract
+        )
+        sign_rep = const.tile([P, 2, ROWS_PASS, HALF_D], BF16)
+        nc.vector.tensor_copy(
+            out=sign_rep[:],
+            in_=sign_f[:].rearrange("n (u w) -> n u w", u=2).unsqueeze(2).to_broadcast([P, 2, ROWS_PASS, HALF_D]),
+        )
+
+        acc = []
+        for half in range(HALVES):
+            acc.append(psum_acc.tile([P, N_TILE], F32, name="acc%d" % half))
+        sign_cols = const.tile([P, K_PASS], BF16)
+        roots_of = {}
+        rows_of = {}
+        banks_of = {}
+        grouped_of = {}
+        codes_of = {}
+        scales_of = {}
+
+        def take_roots(batch):
+            roots = work.tile([P, 2, ROWS, HALF_D], BF16, name="roots%d" % batch, tag="roots")
+            for r in range(ROWS):
+                col = column_of(batch * ROWS + r)
+                nc.scalar.activation(
+                    out=roots[:, :, r, :],
+                    in_=abs_f[:].rearrange("n (u w) -> n u w", u=2),
+                    func=ACT.Sqrt,
+                    bias=eps_scaled[:, 0:1],
+                    scale=abs_scaled[:, col : col + 1],
+                )
+            roots_of[batch] = roots
+
+        def sign_the_rows(batch):
+            rows = work.tile([P, 2, ROWS, HALF_D], BF16, name="rows%d" % batch, tag="rows")
+            for r in range(ROWS):
+                col = column_of(batch * ROWS + r)
+                nc.vector.tensor_scalar_mul(
+                    out=rows[:, :, r, :], in0=roots_of[batch][:, :, r, :], scalar1=sign_f[:, col : col + 1]
+                )
+            rows_of[batch] = rows
+
+        def transpose_words(bank, slot, words, first_row):
+            for u in range(2):
+                nc.tensor.transpose(
+                    bank[:, u, slot, :],
+                    words[:, u, first_row : first_row + ROWS_PASS, :].rearrange("n a w -> n (a w)"),
+                    ident[:],
+                )
+
+        def transpose_batch(batch):
+            words = rows_of[batch][:].bitcast(F32)
+            banks = []
+            for pair in range(BATCH // 2):
+                bank = psum_t.tile([P, 2, 2, P], F32, name="bank%d_%d" % (batch, pair), tag="bank")
+                for slot in range(2):
+                    transpose_words(bank, slot, words, (2 * pair + slot) * ROWS_PASS)
+                banks.append(bank)
+            banks_of[batch] = banks
+
+        def sign_the_columns(batch):
+            grouped = work.tile([P, BATCH, P, 4], BF16, name="grouped%d" % batch, tag="grouped", align_bytes=64)
+            for pair in range(BATCH // 2):
+                nc.vector.tensor_tensor(
+                    out=grouped[:, 2 * pair : 2 * pair + 2, :, :].rearrange("p q n (u e) -> p q n u e", e=2),
+                    in0=banks_of[batch][pair][:].bitcast(BF16).rearrange("p u q (n e) -> p q n u e", e=2),
+                    in1=sign_cols[:]
+                    .rearrange("p (n u e) -> p n u e", u=2, e=2)
+                    .unsqueeze(1)
+                    .to_broadcast([P, 2, P, 2, 2]),
+                    op=ALU.mult,
+                )
+            grouped_of[batch] = grouped
+
+        def quantise(batch):
+            codes = x_pool.tile([P, BATCH * P], U32, name="x_codes%d" % batch, tag="x_codes", align_bytes=64)
+            scales = x_pool.tile([P, BATCH * P], U8, name="x_scales%d" % batch, tag="x_scales", align_bytes=64)
+            nc.vector.quantize_mx(
+                out=codes[:].bitcast(FP8X4),
+                scales=scales[:],
+                in_=grouped_of[batch][:].rearrange("p q n t -> p (q n t)"),
+            )
+            codes_of[batch] = codes
+            scales_of[batch] = scales
+
+        def multiply(batch):
+            for q in range(BATCH):
+                g = batch * BATCH + q
+                for half in range(HALVES):
+                    nc.tensor.matmul_mx(
+                        out=acc[half][:],
+                        lhsT=codes_of[batch][:, q * P : (q + 1) * P].bitcast(FP8X4),
+                        lhsT_scale=scales_of[batch][:, q * P : (q + 1) * P],
+                        rhs=w_words[g // 2][:, g % 2, half * N_TILE : (half + 1) * N_TILE].bitcast(FP8X4),
+                        rhs_scale=w_planes[batch][4 * q : P, half * N_TILE : (half + 1) * N_TILE],
+                        start=(g == 0),
+                        stop=(g == PASSES - 1),
+                    )
+
+        sign_bank = psum_t.tile([P, 2, 2, P], F32, name="sign_bank", tag="bank")
+        transpose_words(sign_bank, 0, sign_rep[:].bitcast(F32), 0)
+
+        for step in range(BATCHES + 3):
+            if step < BATCHES:
+                take_roots(step)
+                sign_the_rows(step)
+                transpose_batch(step)
+            if step == 0:
+                nc.vector.tensor_copy(
+                    out=sign_cols[:].bitcast(F32).rearrange("p (n u) -> p n u", u=2),
+                    in_=sign_bank[:, :, 0, :].rearrange("p u n -> p n u"),
+                )
+            if 1 <= step <= BATCHES:
+                sign_the_columns(step - 1)
+            if 2 <= step <= BATCHES + 1:
+                quantise(step - 2)
+            if step >= 3:
+                multiply(step - 3)
+
+        bias_sb = const.tile([P, C], F32)
+        out_sb = const.tile([P, C], F32)
+        for half in range(HALVES):
+            cols = slice(half * N_TILE, (half + 1) * N_TILE)
+            nc.scalar.copy(out=bias_sb[:, cols], in_=bias_ps[half][:])
+        for half in range(HALVES):
+            cols = slice(half * N_TILE, (half + 1) * N_TILE)
+            nc.vector.tensor_tensor(out=out_sb[:, cols], in0=acc[half][:], in1=bias_sb[:, cols], op=ALU.add)
+            queue = nc.sync if half == 0 else nc.scalar
+            queue.dma_start(out=out[:, cols], in_=out_sb[:, cols])

@@ -63,12 +63,15 @@ def tile_bcnnresnet_k_kernel(tc, feat, W_words, W_scales, b, out):
         nc.vector.memset(ones[:], 1.0)
         nc.scalar.dma_start(out=bias_rows[0:1, :], in_=b.rearrange("(o c) -> o c", o=1))
 
+        ident = const.tile([P, P], F32)
+        make_identity(nc, ident[:])
+
         w_words = []
         for batch in range(BATCHES):
             for quad in range(4):
-                nc.sync.dma_start(
-                    out=w_planes[batch][32 * quad : 32 * quad + 16, :].bitcast(I32),
-                    in_=W_scales[BATCH * batch : BATCH * (batch + 1), 4 * quad : 4 * quad + 4, :].bitcast(I32),
+                nc.gpsimd.dma_start(
+                    out=w_planes[batch][32 * quad : 32 * quad + 16, :].bitcast(F32),
+                    in_=W_scales[BATCH * batch : BATCH * (batch + 1), 4 * quad : 4 * quad + 4, :].bitcast(F32),
                 )
             for pair in range(BATCH // 2):
                 first = BATCH * batch + 2 * pair
@@ -78,9 +81,6 @@ def tile_bcnnresnet_k_kernel(tc, feat, W_words, W_scales, b, out):
                     in_=W_words[first : first + 2].rearrange("g p c t -> p g (c t)").bitcast(I32),
                 )
                 w_words.append(words)
-
-        ident = const.tile([P, P], F32)
-        make_identity(nc, ident[:])
 
         bias_ps = []
         for half in range(HALVES):

@@ -32,10 +32,6 @@ HALF_D = D // 2
 FLOPS = 2 * P * D * D * C
 
 
-def column_of(i):
-    return ((i // 2) % 2) * HALF_D + (i // 4) * 2 + i % 2
-
-
 def tile_bcnnresnet_k_kernel(tc, feat, W_words, W_scales, b, out):
     nc = tc.nc
     with ExitStack() as ctx:
@@ -90,48 +86,52 @@ def tile_bcnnresnet_k_kernel(tc, feat, W_words, W_scales, b, out):
             )
             bias_ps.append(spread)
 
-        f_sorted = const.tile([P, D], F32)
-        nc.vector.tensor_copy(
-            out=f_sorted[:].rearrange("n (u h e) -> n u h e", u=2, e=2),
-            in_=feat_sb[:].rearrange("n (h u e) -> n u h e", u=2, e=2),
-        )
         abs_f = const.tile([P, D], F32)
         abs_sum = const.tile([P, 1], F32)
         nc.vector.scalar_tensor_tensor(
-            out=abs_f[:], in0=f_sorted[:], scalar=-1.0, in1=f_sorted[:], op0=ALU.mult, op1=ALU.max, accum_out=abs_sum[:]
+            out=abs_f[:], in0=feat_sb[:], scalar=-1.0, in1=feat_sb[:], op0=ALU.mult, op1=ALU.max, accum_out=abs_sum[:]
         )
         nonzero = const.tile([P, D], F32)
         count = const.tile([P, 1], F32)
         nc.vector.tensor_scalar(
-            out=nonzero[:], in0=f_sorted[:], scalar1=0.0, scalar2=None, op0=ALU.not_equal, op1=ALU.add, accum_out=count[:]
+            out=nonzero[:], in0=feat_sb[:], scalar1=0.0, scalar2=None, op0=ALU.not_equal, op1=ALU.add, accum_out=count[:]
         )
+        is_neg = const.tile([P, D], F32)
+        nc.vector.tensor_scalar(out=is_neg[:], in0=feat_sb[:], scalar1=0.0, scalar2=None, op0=ALU.is_lt)
         sum_sq = const.tile([P, 1], F32)
         nc.vector.tensor_tensor(out=sum_sq[:], in0=abs_sum[:], in1=abs_sum[:], op=ALU.mult)
         eps_sum = const.tile([P, 1], F32)
         nc.vector.scalar_tensor_tensor(
             out=eps_sum[:], in0=count[:], scalar=EPS_SQRT, in1=count[:], op0=ALU.mult, op1=ALU.mult
         )
+        abs_sorted = const.tile([P, D], F32)
+        nc.vector.tensor_copy(
+            out=abs_sorted[:].rearrange("n (u h e) -> n u h e", u=2, e=2),
+            in_=abs_f[:].rearrange("n (h u e) -> n u h e", u=2, e=2),
+        )
         norm_sq = const.tile([P, 1], F32)
-        nc.vector.tensor_tensor(out=norm_sq[:], in0=sum_sq[:], in1=eps_sum[:], op=ALU.add)
-        norm_sq_clamped = const.tile([P, 1], F32)
-        nc.vector.tensor_scalar_max(out=norm_sq_clamped[:], in0=norm_sq[:], scalar1=EPS_NORM * EPS_NORM)
+        nc.vector.tensor_scalar(
+            out=norm_sq[:], in0=eps_sum[:], scalar1=sum_sq[:, 0:1], scalar2=EPS_NORM * EPS_NORM, op0=ALU.add, op1=ALU.max
+        )
+        sign_f = const.tile([P, D], F32)
+        nc.vector.scalar_tensor_tensor(
+            out=sign_f[:], in0=feat_sb[:], scalar=0.0, in1=is_neg[:], op0=ALU.is_gt, op1=ALU.subtract
+        )
         inv_norm_sq = const.tile([P, 1], F32)
-        nc.vector.reciprocal(out=inv_norm_sq[:], in_=norm_sq_clamped[:])
+        nc.vector.reciprocal(out=inv_norm_sq[:], in_=norm_sq[:])
+        sign_sorted = const.tile([P, D], BF16)
+        nc.vector.tensor_copy(
+            out=sign_sorted[:].rearrange("n (u h e) -> n u h e", u=2, e=2),
+            in_=sign_f[:].rearrange("n (h u e) -> n u h e", u=2, e=2),
+        )
         abs_scaled = const.tile([P, D], F32)
         nc.vector.tensor_scalar_mul(out=abs_scaled[:], in0=abs_f[:], scalar1=inv_norm_sq[:, 0:1])
         eps_scaled = const.tile([P, 1], F32)
         nc.vector.tensor_scalar_mul(out=eps_scaled[:], in0=inv_norm_sq[:], scalar1=EPS_SQRT)
-
-        is_neg = const.tile([P, D], F32)
-        nc.vector.tensor_scalar(out=is_neg[:], in0=f_sorted[:], scalar1=0.0, scalar2=None, op0=ALU.is_lt)
-        sign_f = const.tile([P, D], F32)
-        nc.vector.scalar_tensor_tensor(
-            out=sign_f[:], in0=f_sorted[:], scalar=0.0, in1=is_neg[:], op0=ALU.is_gt, op1=ALU.subtract
-        )
         sign_rep = const.tile([P, 2, ROWS_PASS, HALF_D], BF16)
         nc.vector.tensor_copy(
             out=sign_rep[:],
-            in_=sign_f[:].rearrange("n (u w) -> n u w", u=2).unsqueeze(2).to_broadcast([P, 2, ROWS_PASS, HALF_D]),
+            in_=sign_sorted[:].rearrange("n (u w) -> n u w", u=2).unsqueeze(2).to_broadcast([P, 2, ROWS_PASS, HALF_D]),
         )
 
         acc = []
@@ -148,22 +148,22 @@ def tile_bcnnresnet_k_kernel(tc, feat, W_words, W_scales, b, out):
         def take_roots(batch):
             roots = work.tile([P, 2, ROWS, HALF_D], BF16, name="roots%d" % batch, tag="roots")
             for r in range(ROWS):
-                col = column_of(batch * ROWS + r)
+                i = batch * ROWS + r
                 nc.scalar.activation(
                     out=roots[:, :, r, :],
-                    in_=abs_f[:].rearrange("n (u w) -> n u w", u=2),
+                    in_=abs_sorted[:].rearrange("n (u w) -> n u w", u=2),
                     func=ACT.Sqrt,
                     bias=eps_scaled[:, 0:1],
-                    scale=abs_scaled[:, col : col + 1],
+                    scale=abs_scaled[:, i : i + 1],
                 )
             roots_of[batch] = roots
 
         def sign_the_rows(batch):
             rows = work.tile([P, 2, ROWS, HALF_D], BF16, name="rows%d" % batch, tag="rows")
             for r in range(ROWS):
-                col = column_of(batch * ROWS + r)
+                i = batch * ROWS + r
                 nc.vector.tensor_scalar_mul(
-                    out=rows[:, :, r, :], in0=roots_of[batch][:, :, r, :], scalar1=sign_f[:, col : col + 1]
+                    out=rows[:, :, r, :], in0=roots_of[batch][:, :, r, :], scalar1=sign_f[:, i : i + 1]
                 )
             rows_of[batch] = rows
 
@@ -202,11 +202,13 @@ def tile_bcnnresnet_k_kernel(tc, feat, W_words, W_scales, b, out):
         def quantise(batch):
             codes = x_pool.tile([P, BATCH * P], U32, name="x_codes%d" % batch, tag="x_codes", align_bytes=64)
             scales = x_pool.tile([P, BATCH * P], U8, name="x_scales%d" % batch, tag="x_scales", align_bytes=64)
-            nc.vector.quantize_mx(
-                out=codes[:].bitcast(FP8X4),
-                scales=scales[:],
-                in_=grouped_of[batch][:].rearrange("p q n t -> p (q n t)"),
-            )
+            for pair in range(BATCH // 2):
+                cols = slice(2 * pair * P, 2 * (pair + 1) * P)
+                nc.vector.quantize_mx(
+                    out=codes[:, cols].bitcast(FP8X4),
+                    scales=scales[:, cols],
+                    in_=grouped_of[batch][:, 2 * pair : 2 * pair + 2, :, :].rearrange("p q n t -> p (q n t)"),
+                )
             codes_of[batch] = codes
             scales_of[batch] = scales
 
@@ -227,10 +229,13 @@ def tile_bcnnresnet_k_kernel(tc, feat, W_words, W_scales, b, out):
         sign_bank = psum_t.tile([P, 2, 2, P], F32, name="sign_bank", tag="bank")
         transpose_words(sign_bank, 0, sign_rep[:].bitcast(F32), 0)
 
-        for step in range(BATCHES + 3):
+        for step in range(BATCHES + 2):
             if step < BATCHES:
                 take_roots(step)
                 sign_the_rows(step)
+            if step >= 2:
+                multiply(step - 2)
+            if step < BATCHES:
                 transpose_batch(step)
             if step == 0:
                 nc.vector.tensor_copy(
@@ -239,10 +244,7 @@ def tile_bcnnresnet_k_kernel(tc, feat, W_words, W_scales, b, out):
                 )
             if 1 <= step <= BATCHES:
                 sign_the_columns(step - 1)
-            if 2 <= step <= BATCHES + 1:
-                quantise(step - 2)
-            if step >= 3:
-                multiply(step - 3)
+                quantise(step - 1)
 
         bias_sb = const.tile([P, C], F32)
         out_sb = const.tile([P, C], F32)

@@ -28,6 +28,7 @@ BATCH = 4
 BATCHES = PASSES // BATCH
 ROWS = BATCH * ROWS_PASS
 HALF_D = D // 2
+SYNC_BATCHES = 2
 
 FLOPS = 2 * P * D * D * C
 
@@ -48,11 +49,13 @@ def tile_bcnnresnet_k_kernel(tc, feat, W_words, W_scales, b, out):
         feat_sb = const.tile([P, D], BF16)
         nc.sync.dma_start(out=feat_sb[:], in_=feat)
 
-        w_planes = []
-        for batch in range(BATCHES):
+        sync_batches = list(range(BATCHES - SYNC_BATCHES, BATCHES))
+        gpsimd_batches = list(range(BATCHES - SYNC_BATCHES))
+        w_planes = {}
+        for batch in sync_batches + gpsimd_batches:
             planes = plane_pool.tile([P, C], U8, name="w_planes%d" % batch, tag="w_planes", align_bytes=64)
             nc.vector.memset(planes[:].bitcast(I32), 0)
-            w_planes.append(planes)
+            w_planes[batch] = planes
         bias_rows = const.tile([P, C], BF16)
         nc.vector.memset(bias_rows[:], 0.0)
         ones = const.tile([P, P], BF16)
@@ -62,21 +65,30 @@ def tile_bcnnresnet_k_kernel(tc, feat, W_words, W_scales, b, out):
         ident = const.tile([P, P], F32)
         make_identity(nc, ident[:])
 
-        w_words = []
-        for batch in range(BATCHES):
+        def load_scales(queue, view, batch, quad):
+            queue.dma_start(
+                out=w_planes[batch][32 * quad : 32 * quad + 16, :].bitcast(view),
+                in_=W_scales[BATCH * batch : BATCH * (batch + 1), 4 * quad : 4 * quad + 4, :].bitcast(view),
+            )
+
+        for batch in gpsimd_batches:
             for quad in range(4):
-                nc.gpsimd.dma_start(
-                    out=w_planes[batch][32 * quad : 32 * quad + 16, :].bitcast(F32),
-                    in_=W_scales[BATCH * batch : BATCH * (batch + 1), 4 * quad : 4 * quad + 4, :].bitcast(F32),
-                )
-            for pair in range(BATCH // 2):
-                first = BATCH * batch + 2 * pair
-                words = w_pool.tile([P, 2, C], U32, name="w_words%d" % (first // 2), tag="w_words", align_bytes=64)
-                nc.sync.dma_start(
-                    out=words[:].bitcast(I32),
-                    in_=W_words[first : first + 2].rearrange("g p c t -> p g (c t)").bitcast(I32),
-                )
-                w_words.append(words)
+                load_scales(nc.gpsimd, F32, batch, quad)
+
+        w_words = []
+        for pair in range(PASSES // 2):
+            words = w_pool.tile([P, 2, C], U32, name="w_words%d" % pair, tag="w_words", align_bytes=64)
+            source = W_words[2 * pair : 2 * pair + 2].rearrange("g p c t -> p g (c t)").bitcast(I32)
+            if pair < PASSES // 2 - 1:
+                nc.sync.dma_start(out=words[:].bitcast(I32), in_=source)
+            else:
+                nc.sync.dma_start(out=words[:, 0, :].bitcast(I32), in_=source[:, 0, :])
+                for half in range(HALVES):
+                    cols = slice(half * N_TILE, (half + 1) * N_TILE)
+                    nc.sync.dma_start(out=words[:, 1, cols].bitcast(I32), in_=source[:, 1, cols])
+            w_words.append(words)
+            if pair < 4 * SYNC_BATCHES:
+                load_scales(nc.sync, I32, sync_batches[pair // 4], pair % 4)
 
         bias_ps = []
         for half in range(HALVES):

@@ -140,6 +140,8 @@ def tile_bcnnresnet_k_kernel(tc, feat, W_words, W_scales, b, out):
         nc.vector.tensor_scalar_mul(out=abs_scaled[:], in0=abs_f[:], scalar1=inv_norm_sq[:, 0:1])
         eps_scaled = const.tile([P, 1], F32)
         nc.vector.tensor_scalar_mul(out=eps_scaled[:], in0=inv_norm_sq[:], scalar1=EPS_SQRT)
+        sign_pairs = const.tile([P, D, 2], BF16)
+        nc.vector.tensor_copy(out=sign_pairs[:], in_=sign_f[:].unsqueeze(2).to_broadcast([P, D, 2]))
         sign_rep = const.tile([P, 2, ROWS_PASS, HALF_D], BF16)
         nc.vector.tensor_copy(
             out=sign_rep[:],
@@ -172,10 +174,14 @@ def tile_bcnnresnet_k_kernel(tc, feat, W_words, W_scales, b, out):
 
         def sign_the_rows(batch):
             rows = work.tile([P, 2, ROWS, HALF_D], BF16, name="rows%d" % batch, tag="rows")
-            for r in range(ROWS):
-                i = batch * ROWS + r
-                nc.vector.tensor_scalar_mul(
-                    out=rows[:, :, r, :], in0=roots_of[batch][:, :, r, :], scalar1=sign_f[:, i : i + 1]
+            for u in range(2):
+                nc.vector.tensor_tensor(
+                    out=rows[:, u, :, :].rearrange("n r (w e) -> n r w e", e=2),
+                    in0=roots_of[batch][:, u, :, :].rearrange("n r (w e) -> n r w e", e=2),
+                    in1=sign_pairs[:, batch * ROWS : (batch + 1) * ROWS, :]
+                    .unsqueeze(2)
+                    .to_broadcast([P, ROWS, HALF_D // 2, 2]),
+                    op=ALU.mult,
                 )
             rows_of[batch] = rows
 

@@ -30,6 +30,8 @@ ROWS = BATCH * ROWS_PASS
 HALF_D = D // 2
 SYNC_BATCHES = 2
 
+TAIL_BLOCKS = ((0, 512), (512, 256), (768, 128), (896, 128))
+
 FLOPS = 2 * P * D * D * C
 
 
@@ -37,7 +39,7 @@ def tile_bcnnresnet_k_kernel(tc, feat, W_words, W_scales, b, out):
     nc = tc.nc
     with ExitStack() as ctx:
         const = ctx.enter_context(tc.tile_pool(name="const", bufs=1))
-        w_pool = ctx.enter_context(tc.tile_pool(name="w_pool", bufs=PASSES // 2))
+        w_pool = ctx.enter_context(tc.tile_pool(name="w_pool", bufs=(PASSES - BATCH) // 2))
         plane_pool = ctx.enter_context(tc.tile_pool(name="plane_pool", bufs=BATCHES))
         x_pool = ctx.enter_context(tc.tile_pool(name="x_pool", bufs=BATCHES))
         work = ctx.enter_context(tc.tile_pool(name="work", bufs=3))
@@ -76,19 +78,19 @@ def tile_bcnnresnet_k_kernel(tc, feat, W_words, W_scales, b, out):
                 load_scales(nc.gpsimd, F32, batch, quad)
 
         w_words = []
-        for pair in range(PASSES // 2):
+        for pair in range((PASSES - BATCH) // 2):
             words = w_pool.tile([P, 2, C], U32, name="w_words%d" % pair, tag="w_words", align_bytes=64)
             source = W_words[2 * pair : 2 * pair + 2].rearrange("g p c t -> p g (c t)").bitcast(I32)
-            if pair < PASSES // 2 - 1:
-                nc.sync.dma_start(out=words[:].bitcast(I32), in_=source)
-            else:
-                nc.sync.dma_start(out=words[:, 0, :].bitcast(I32), in_=source[:, 0, :])
-                for half in range(HALVES):
-                    cols = slice(half * N_TILE, (half + 1) * N_TILE)
-                    nc.sync.dma_start(out=words[:, 1, cols].bitcast(I32), in_=source[:, 1, cols])
+            nc.sync.dma_start(out=words[:].bitcast(I32), in_=source)
             w_words.append(words)
             if pair < 4 * SYNC_BATCHES:
                 load_scales(nc.sync, I32, sync_batches[pair // 4], pair % 4)
+        w_last = const.tile([P, BATCH, C], U32, align_bytes=64)
+        last_source = W_words[PASSES - BATCH : PASSES].rearrange("g p c t -> p g (c t)").bitcast(I32)
+        for first, width in TAIL_BLOCKS:
+            nc.sync.dma_start(
+                out=w_last[:, :, first : first + width].bitcast(I32), in_=last_source[:, :, first : first + width]
+            )
 
         bias_ps = []
         for half in range(HALVES):
@@ -241,13 +243,13 @@ def tile_bcnnresnet_k_kernel(tc, feat, W_words, W_scales, b, out):
                         rhs=w_words[g // 2][:, g % 2, half * N_TILE : (half + 1) * N_TILE].bitcast(FP8X4),
                         rhs_scale=w_planes[batch][4 * q : P, half * N_TILE : (half + 1) * N_TILE],
                         start=(g == 0),
-                        stop=(g == PASSES - 1),
+                        stop=(g == PASSES - BATCH - 1),
                     )
 
         sign_bank = psum_t.tile([P, 2, 2, P], F32, name="sign_bank", tag="bank")
         transpose_words(sign_bank, 0, sign_rep[:].bitcast(F32), 0)
 
-        for step in range(BATCHES + 2):
+        for step in range(BATCHES + 1):
             if step < BATCHES:
                 take_roots(step)
                 sign_the_rows(step)
@@ -269,8 +271,25 @@ def tile_bcnnresnet_k_kernel(tc, feat, W_words, W_scales, b, out):
         for half in range(HALVES):
             cols = slice(half * N_TILE, (half + 1) * N_TILE)
             nc.scalar.copy(out=bias_sb[:, cols], in_=bias_ps[half][:])
+        partial = const.tile([P, C], F32)
         for half in range(HALVES):
             cols = slice(half * N_TILE, (half + 1) * N_TILE)
-            nc.vector.tensor_tensor(out=out_sb[:, cols], in0=acc[half][:], in1=bias_sb[:, cols], op=ALU.add)
-            queue = nc.sync if half == 0 else nc.scalar
+            nc.vector.tensor_tensor(out=partial[:, cols], in0=acc[half][:], in1=bias_sb[:, cols], op=ALU.add)
+        last = BATCHES - 1
+        for index, (first, width) in enumerate(TAIL_BLOCKS):
+            cols = slice(first, first + width)
+            bank = psum_t.tile([P, 2, 2, P], F32, name="tail%d" % index, tag="bank")
+            tail = bank[:].rearrange("p a b n -> p (a b n)")[:, 0:width]
+            for q in range(BATCH):
+                nc.tensor.matmul_mx(
+                    out=tail,
+                    lhsT=codes_of[last][:, q * P : (q + 1) * P].bitcast(FP8X4),
+                    lhsT_scale=scales_of[last][:, q * P : (q + 1) * P],
+                    rhs=w_last[:, q, cols].bitcast(FP8X4),
+                    rhs_scale=w_planes[last][4 * q : P, cols],
+                    start=(q == 0),
+                    stop=(q == BATCH - 1),
+                )
+            nc.vector.tensor_tensor(out=out_sb[:, cols], in0=tail, in1=partial[:, cols], op=ALU.add)
+            queue = nc.scalar if index % 2 == 0 else nc.sync
             queue.dma_start(out=out[:, cols], in_=out_sb[:, cols])

@@ -87,9 +87,16 @@ def tile_bcnnresnet_k_kernel(tc, feat, W_words, W_scales, b, out):
                 load_scales(nc.sync, I32, sync_batches[pair // 4], pair % 4)
         w_last = const.tile([P, BATCH, C], U32, align_bytes=64)
         last_source = W_words[PASSES - BATCH : PASSES].rearrange("g p c t -> p g (c t)").bitcast(I32)
-        for first, width in TAIL_BLOCKS:
+        for low, count, first, width in (
+            (0, BATCH, 0, 512),
+            (0, BATCH, 512, 256),
+            (0, BATCH - 1, 768, 256),
+            (BATCH - 1, 1, 768, 128),
+            (BATCH - 1, 1, 896, 128),
+        ):
             nc.sync.dma_start(
-                out=w_last[:, :, first : first + width].bitcast(I32), in_=last_source[:, :, first : first + width]
+                out=w_last[:, low : low + count, first : first + width].bitcast(I32),
+                in_=last_source[:, low : low + count, first : first + width],
             )
 
         bias_ps = []
@@ -276,20 +283,37 @@ def tile_bcnnresnet_k_kernel(tc, feat, W_words, W_scales, b, out):
             cols = slice(half * N_TILE, (half + 1) * N_TILE)
             nc.vector.tensor_tensor(out=partial[:, cols], in0=acc[half][:], in1=bias_sb[:, cols], op=ALU.add)
         last = BATCHES - 1
-        for index, (first, width) in enumerate(TAIL_BLOCKS):
-            cols = slice(first, first + width)
+        tails = []
+        for index in range(len(TAIL_BLOCKS)):
             bank = psum_t.tile([P, 2, 2, P], F32, name="tail%d" % index, tag="bank")
-            tail = bank[:].rearrange("p a b n -> p (a b n)")[:, 0:width]
-            for q in range(BATCH):
-                nc.tensor.matmul_mx(
-                    out=tail,
-                    lhsT=codes_of[last][:, q * P : (q + 1) * P].bitcast(FP8X4),
-                    lhsT_scale=scales_of[last][:, q * P : (q + 1) * P],
-                    rhs=w_last[:, q, cols].bitcast(FP8X4),
-                    rhs_scale=w_planes[last][4 * q : P, cols],
-                    start=(q == 0),
-                    stop=(q == BATCH - 1),
-                )
-            nc.vector.tensor_tensor(out=out_sb[:, cols], in0=tail, in1=partial[:, cols], op=ALU.add)
+            tails.append(bank[:].rearrange("p a b n -> p (a b n)")[:, 0 : TAIL_BLOCKS[index][1]])
+
+        def multiply_tail(index, q):
+            first, width = TAIL_BLOCKS[index]
+            nc.tensor.matmul_mx(
+                out=tails[index],
+                lhsT=codes_of[last][:, q * P : (q + 1) * P].bitcast(FP8X4),
+                lhsT_scale=scales_of[last][:, q * P : (q + 1) * P],
+                rhs=w_last[:, q, first : first + width].bitcast(FP8X4),
+                rhs_scale=w_planes[last][4 * q : P, first : first + width],
+                start=(q == 0),
+                stop=(q == BATCH - 1),
+            )
+
+        def finish_tail(index):
+            first, width = TAIL_BLOCKS[index]
+            cols = slice(first, first + width)
+            nc.vector.tensor_tensor(out=out_sb[:, cols], in0=tails[index], in1=partial[:, cols], op=ALU.add)
             queue = nc.scalar if index % 2 == 0 else nc.sync
             queue.dma_start(out=out[:, cols], in_=out_sb[:, cols])
+
+        for index in (0, 1):
+            for q in range(BATCH):
+                multiply_tail(index, q)
+            finish_tail(index)
+        for q in range(BATCH - 1):
+            for index in (2, 3):
+                multiply_tail(index, q)
+        for index in (2, 3):
+            multiply_tail(index, BATCH - 1)
+            finish_tail(index)

from contextlib import ExitStack

import concourse.mybir as mybir
from concourse.masks import make_identity

F32 = mybir.dt.float32
BF16 = mybir.dt.bfloat16
I32 = mybir.dt.int32
U32 = mybir.dt.uint32
U8 = mybir.dt.uint8
FP8X4 = mybir.dt.float8_e4m3fn_x4
ALU = mybir.AluOpType
ACT = mybir.ActivationFunctionType
AX = mybir.AxisListType

P = 128
D = 128
C = 1024
EPS_SQRT = 1e-10
EPS_NORM = 1e-12

K_PASS = 512
ROWS_PASS = K_PASS // D
PASSES = D * D // K_PASS
N_TILE = 512
HALVES = C // N_TILE
BATCH = 4
BATCHES = PASSES // BATCH
ROWS = BATCH * ROWS_PASS
HALF_D = D // 2
SYNC_BATCHES = 2

TAIL_BLOCKS = ((0, 512), (512, 256), (768, 128), (896, 128))

FLOPS = 2 * P * D * D * C


def tile_bcnnresnet_k_kernel(tc, feat, W_words, W_scales, b, out):
    nc = tc.nc
    with ExitStack() as ctx:
        const = ctx.enter_context(tc.tile_pool(name="const", bufs=1))
        w_pool = ctx.enter_context(tc.tile_pool(name="w_pool", bufs=(PASSES - BATCH) // 2))
        plane_pool = ctx.enter_context(tc.tile_pool(name="plane_pool", bufs=BATCHES))
        x_pool = ctx.enter_context(tc.tile_pool(name="x_pool", bufs=BATCHES))
        work = ctx.enter_context(tc.tile_pool(name="work", bufs=3))
        psum_acc = ctx.enter_context(tc.psum_pool(name="psum_acc", bufs=1))
        psum_bias = ctx.enter_context(tc.psum_pool(name="psum_bias", bufs=HALVES))
        psum_t = ctx.enter_context(tc.psum_pool(name="psum_t", bufs=4))
        ctx.enter_context(tc.manual_schedule())

        feat_sb = const.tile([P, D], BF16)
        nc.sync.dma_start(out=feat_sb[:], in_=feat)

        sync_batches = list(range(BATCHES - SYNC_BATCHES, BATCHES))
        gpsimd_batches = list(range(BATCHES - SYNC_BATCHES))
        w_planes = {}
        for batch in sync_batches + gpsimd_batches:
            planes = plane_pool.tile([P, C], U8, name="w_planes%d" % batch, tag="w_planes", align_bytes=64)
            nc.vector.memset(planes[:].bitcast(I32), 0)
            w_planes[batch] = planes
        bias_rows = const.tile([P, C], BF16)
        nc.vector.memset(bias_rows[:], 0.0)
        ones = const.tile([P, P], BF16)
        nc.vector.memset(ones[:], 1.0)
        nc.scalar.dma_start(out=bias_rows[0:1, :], in_=b.rearrange("(o c) -> o c", o=1))

        ident = const.tile([P, P], F32)
        make_identity(nc, ident[:])

        def load_scales(queue, view, batch, quad):
            queue.dma_start(
                out=w_planes[batch][32 * quad : 32 * quad + 16, :].bitcast(view),
                in_=W_scales[BATCH * batch : BATCH * (batch + 1), 4 * quad : 4 * quad + 4, :].bitcast(view),
            )

        for batch in gpsimd_batches:
            for quad in range(4):
                load_scales(nc.gpsimd, F32, batch, quad)

        w_words = []
        for pair in range((PASSES - BATCH) // 2):
            words = w_pool.tile([P, 2, C], U32, name="w_words%d" % pair, tag="w_words", align_bytes=64)
            source = W_words[2 * pair : 2 * pair + 2].rearrange("g p c t -> p g (c t)").bitcast(I32)
            nc.sync.dma_start(out=words[:].bitcast(I32), in_=source)
            w_words.append(words)
            if pair < 4 * SYNC_BATCHES:
                load_scales(nc.sync, I32, sync_batches[pair // 4], pair % 4)
        w_last = const.tile([P, BATCH, C], U32, align_bytes=64)
        last_source = W_words[PASSES - BATCH : PASSES].rearrange("g p c t -> p g (c t)").bitcast(I32)
        for low, count, first, width in (
            (0, BATCH, 0, 512),
            (0, BATCH, 512, 256),
            (0, BATCH - 1, 768, 256),
            (BATCH - 1, 1, 768, 128),
            (BATCH - 1, 1, 896, 128),
        ):
            nc.sync.dma_start(
                out=w_last[:, low : low + count, first : first + width].bitcast(I32),
                in_=last_source[:, low : low + count, first : first + width],
            )

        bias_ps = []
        for half in range(HALVES):
            spread = psum_bias.tile([P, N_TILE], F32, name="bias_ps%d" % half, tag="bias_ps")
            nc.tensor.matmul(
                out=spread[:], lhsT=ones[:], rhs=bias_rows[:, half * N_TILE : (half + 1) * N_TILE], start=True, stop=True
            )
            bias_ps.append(spread)

        abs_f = const.tile([P, D], F32)
        abs_sum = const.tile([P, 1], F32)
        nc.vector.scalar_tensor_tensor(
            out=abs_f[:], in0=feat_sb[:], scalar=-1.0, in1=feat_sb[:], op0=ALU.mult, op1=ALU.max, accum_out=abs_sum[:]
        )
        nonzero = const.tile([P, D], F32)
        count = const.tile([P, 1], F32)
        nc.vector.tensor_scalar(
            out=nonzero[:], in0=feat_sb[:], scalar1=0.0, scalar2=None, op0=ALU.not_equal, op1=ALU.add, accum_out=count[:]
        )
        is_neg = const.tile([P, D], F32)
        nc.vector.tensor_scalar(out=is_neg[:], in0=feat_sb[:], scalar1=0.0, scalar2=None, op0=ALU.is_lt)
        sum_sq = const.tile([P, 1], F32)
        nc.vector.tensor_tensor(out=sum_sq[:], in0=abs_sum[:], in1=abs_sum[:], op=ALU.mult)
        eps_sum = const.tile([P, 1], F32)
        nc.vector.scalar_tensor_tensor(
            out=eps_sum[:], in0=count[:], scalar=EPS_SQRT, in1=count[:], op0=ALU.mult, op1=ALU.mult
        )
        abs_sorted = const.tile([P, D], F32)
        nc.vector.tensor_copy(
            out=abs_sorted[:].rearrange("n (u h e) -> n u h e", u=2, e=2),
            in_=abs_f[:].rearrange("n (h u e) -> n u h e", u=2, e=2),
        )
        norm_sq = const.tile([P, 1], F32)
        nc.vector.tensor_scalar(
            out=norm_sq[:], in0=eps_sum[:], scalar1=sum_sq[:, 0:1], scalar2=EPS_NORM * EPS_NORM, op0=ALU.add, op1=ALU.max
        )
        sign_f = const.tile([P, D], F32)
        nc.vector.scalar_tensor_tensor(
            out=sign_f[:], in0=feat_sb[:], scalar=0.0, in1=is_neg[:], op0=ALU.is_gt, op1=ALU.subtract
        )
        inv_norm_sq = const.tile([P, 1], F32)
        nc.vector.reciprocal(out=inv_norm_sq[:], in_=norm_sq[:])
        sign_sorted = const.tile([P, D], BF16)
        nc.vector.tensor_copy(
            out=sign_sorted[:].rearrange("n (u h e) -> n u h e", u=2, e=2),
            in_=sign_f[:].rearrange("n (h u e) -> n u h e", u=2, e=2),
        )
        abs_scaled = const.tile([P, D], F32)
        nc.vector.tensor_scalar_mul(out=abs_scaled[:], in0=abs_f[:], scalar1=inv_norm_sq[:, 0:1])
        eps_scaled = const.tile([P, 1], F32)
        nc.vector.tensor_scalar_mul(out=eps_scaled[:], in0=inv_norm_sq[:], scalar1=EPS_SQRT)
        sign_pairs = const.tile([P, D, 2], BF16)
        nc.vector.tensor_copy(out=sign_pairs[:], in_=sign_f[:].unsqueeze(2).to_broadcast([P, D, 2]))
        sign_rep = const.tile([P, 2, ROWS_PASS, HALF_D], BF16)
        nc.vector.tensor_copy(
            out=sign_rep[:],
            in_=sign_sorted[:].rearrange("n (u w) -> n u w", u=2).unsqueeze(2).to_broadcast([P, 2, ROWS_PASS, HALF_D]),
        )

        acc = []
        for half in range(HALVES):
            acc.append(psum_acc.tile([P, N_TILE], F32, name="acc%d" % half))
        sign_cols = const.tile([P, K_PASS], BF16)
        roots_of = {}
        rows_of = {}
        banks_of = {}
        grouped_of = {}
        codes_of = {}
        scales_of = {}

        def take_roots(batch):
            roots = work.tile([P, 2, ROWS, HALF_D], BF16, name="roots%d" % batch, tag="roots")
            for r in range(ROWS):
                i = batch * ROWS + r
                nc.scalar.activation(
                    out=roots[:, :, r, :],
                    in_=abs_sorted[:].rearrange("n (u w) -> n u w", u=2),
                    func=ACT.Sqrt,
                    bias=eps_scaled[:, 0:1],
                    scale=abs_scaled[:, i : i + 1],
                )
            roots_of[batch] = roots

        def sign_the_rows(batch):
            rows = work.tile([P, 2, ROWS, HALF_D], BF16, name="rows%d" % batch, tag="rows")
            for u in range(2):
                nc.vector.tensor_tensor(
                    out=rows[:, u, :, :].rearrange("n r (w e) -> n r w e", e=2),
                    in0=roots_of[batch][:, u, :, :].rearrange("n r (w e) -> n r w e", e=2),
                    in1=sign_pairs[:, batch * ROWS : (batch + 1) * ROWS, :]
                    .unsqueeze(2)
                    .to_broadcast([P, ROWS, HALF_D // 2, 2]),
                    op=ALU.mult,
                )
            rows_of[batch] = rows

        def transpose_words(bank, slot, words, first_row):
            for u in range(2):
                nc.tensor.transpose(
                    bank[:, u, slot, :],
                    words[:, u, first_row : first_row + ROWS_PASS, :].rearrange("n a w -> n (a w)"),
                    ident[:],
                )

        def transpose_batch(batch):
            words = rows_of[batch][:].bitcast(F32)
            banks = []
            for pair in range(BATCH // 2):
                bank = psum_t.tile([P, 2, 2, P], F32, name="bank%d_%d" % (batch, pair), tag="bank")
                for slot in range(2):
                    transpose_words(bank, slot, words, (2 * pair + slot) * ROWS_PASS)
                banks.append(bank)
            banks_of[batch] = banks

        def sign_the_columns(batch):
            grouped = work.tile([P, BATCH, P, 4], BF16, name="grouped%d" % batch, tag="grouped", align_bytes=64)
            for pair in range(BATCH // 2):
                nc.vector.tensor_tensor(
                    out=grouped[:, 2 * pair : 2 * pair + 2, :, :].rearrange("p q n (u e) -> p q n u e", e=2),
                    in0=banks_of[batch][pair][:].bitcast(BF16).rearrange("p u q (n e) -> p q n u e", e=2),
                    in1=sign_cols[:]
                    .rearrange("p (n u e) -> p n u e", u=2, e=2)
                    .unsqueeze(1)
                    .to_broadcast([P, 2, P, 2, 2]),
                    op=ALU.mult,
                )
            grouped_of[batch] = grouped

        def quantise(batch):
            codes = x_pool.tile([P, BATCH * P], U32, name="x_codes%d" % batch, tag="x_codes", align_bytes=64)
            scales = x_pool.tile([P, BATCH * P], U8, name="x_scales%d" % batch, tag="x_scales", align_bytes=64)
            for pair in range(BATCH // 2):
                cols = slice(2 * pair * P, 2 * (pair + 1) * P)
                nc.vector.quantize_mx(
                    out=codes[:, cols].bitcast(FP8X4),
                    scales=scales[:, cols],
                    in_=grouped_of[batch][:, 2 * pair : 2 * pair + 2, :, :].rearrange("p q n t -> p (q n t)"),
                )
            codes_of[batch] = codes
            scales_of[batch] = scales

        def multiply(batch):
            for q in range(BATCH):
                g = batch * BATCH + q
                for half in range(HALVES):
                    nc.tensor.matmul_mx(
                        out=acc[half][:],
                        lhsT=codes_of[batch][:, q * P : (q + 1) * P].bitcast(FP8X4),
                        lhsT_scale=scales_of[batch][:, q * P : (q + 1) * P],
                        rhs=w_words[g // 2][:, g % 2, half * N_TILE : (half + 1) * N_TILE].bitcast(FP8X4),
                        rhs_scale=w_planes[batch][4 * q : P, half * N_TILE : (half + 1) * N_TILE],
                        start=(g == 0),
                        stop=(g == PASSES - BATCH - 1),
                    )

        sign_bank = psum_t.tile([P, 2, 2, P], F32, name="sign_bank", tag="bank")
        transpose_words(sign_bank, 0, sign_rep[:].bitcast(F32), 0)

        for step in range(BATCHES + 1):
            if step < BATCHES:
                take_roots(step)
                sign_the_rows(step)
            if step >= 2:
                multiply(step - 2)
            if step < BATCHES:
                transpose_batch(step)
            if step == 0:
                nc.vector.tensor_copy(
                    out=sign_cols[:].bitcast(F32).rearrange("p (n u) -> p n u", u=2),
                    in_=sign_bank[:, :, 0, :].rearrange("p u n -> p n u"),
                )
            if 1 <= step <= BATCHES:
                sign_the_columns(step - 1)
                quantise(step - 1)

        bias_sb = const.tile([P, C], F32)
        out_sb = const.tile([P, C], F32)
        for half in range(HALVES):
            cols = slice(half * N_TILE, (half + 1) * N_TILE)
            nc.scalar.copy(out=bias_sb[:, cols], in_=bias_ps[half][:])
        partial = const.tile([P, C], F32)
        for half in range(HALVES):
            cols = slice(half * N_TILE, (half + 1) * N_TILE)
            nc.vector.tensor_tensor(out=partial[:, cols], in0=acc[half][:], in1=bias_sb[:, cols], op=ALU.add)
        last = BATCHES - 1
        tails = []
        for index in range(len(TAIL_BLOCKS)):
            bank = psum_t.tile([P, 2, 2, P], F32, name="tail%d" % index, tag="bank")
            tails.append(bank[:].rearrange("p a b n -> p (a b n)")[:, 0 : TAIL_BLOCKS[index][1]])

        def multiply_tail(index, q):
            first, width = TAIL_BLOCKS[index]
            nc.tensor.matmul_mx(
                out=tails[index],
                lhsT=codes_of[last][:, q * P : (q + 1) * P].bitcast(FP8X4),
                lhsT_scale=scales_of[last][:, q * P : (q + 1) * P],
                rhs=w_last[:, q, first : first + width].bitcast(FP8X4),
                rhs_scale=w_planes[last][4 * q : P, first : first + width],
                start=(q == 0),
                stop=(q == BATCH - 1),
            )

        def finish_tail(index):
            first, width = TAIL_BLOCKS[index]
            cols = slice(first, first + width)
            nc.vector.tensor_tensor(out=out_sb[:, cols], in0=tails[index], in1=partial[:, cols], op=ALU.add)
            queue = nc.scalar if index % 2 == 0 else nc.sync
            queue.dma_start(out=out[:, cols], in_=out_sb[:, cols])

        for index in (0, 1):
            for q in range(BATCH):
                multiply_tail(index, q)
            finish_tail(index)
        for q in range(BATCH - 1):
            for index in (2, 3):
                multiply_tail(index, q)
        for index in (2, 3):
            multiply_tail(index, BATCH - 1)
            finish_tail(index)
